import numpy as np
import ml_dtypes


def mxq(x, axis, fmt="e4m3"):
    dtype, down = {"e4m3": (ml_dtypes.float8_e4m3fn, 7), "e5m2": (ml_dtypes.float8_e5m2, 14)}[fmt]
    v = np.moveaxis(np.asarray(x, np.float32).astype(ml_dtypes.bfloat16).astype(np.float64), axis, -1)
    blocks = v.reshape(v.shape[:-1] + (-1, 32))
    amax = np.abs(blocks).max(-1, keepdims=True)
    byte = np.maximum(np.where(amax > 0, np.frexp(amax)[1] - 1 + 127, 0) - down, 1)
    scale = np.exp2(byte - 127.0)
    codes = (blocks / scale).astype(np.float32).astype(dtype).astype(np.float64)
    return np.moveaxis((codes * scale).reshape(v.shape), -1, axis)


WIDE = False


def mx_kscale(k):
    if not WIDE:
        return np.ones(k)
    levels = np.array([10, -10, 5, -5, 0])
    a = np.random.permutation(np.resize(levels, k // 512 * 4)).reshape(k // 512, 4)
    idx = np.arange(k)
    return np.exp2(a[idx // 512, idx % 128 // 32])


BF16 = ml_dtypes.bfloat16


def bf(x):
    return np.asarray(x, np.float32).astype(BF16)


def f64(x):
    return np.asarray(x).astype(np.float64)


B, CK, CV, NO, T, H, W = 1, 128, 512, 3, 4, 32, 16
N = T * H * W
P = H * W
C = NO * CV


def setup_inputs():
    s = mx_kscale(N)
    g = np.exp2(np.round(np.log2(np.mean(s))))
    mk = np.random.standard_normal((B, CK, N))
    qk = np.random.standard_normal((B, CK, P))
    qe = np.random.uniform(0.0, 1.0, (B, CK, P))
    ms = bf(0.75 + 0.5 * np.random.uniform(0.0, 1.0, (B, N)))
    d = (np.log2(np.max(s)) - np.log2(s))[None, :] * np.log(2.0) * np.sqrt(CK) / f64(ms)
    a0 = mk[:, 0, :] ** 2 + d
    mk[:, 0, :] = np.sqrt(a0)
    qk[:, 0, :] = 0.0
    qe[:, 0, :] = 1.0
    mk, qk, qe = bf(mk), bf(qk), bf(qe)
    mksq = f64(mk) * f64(mk)
    mksq[:, 0, :] = a0
    return {"memory_key": mk,
            "memory_key_sq": bf(mksq),
            "query_key": qk,
            "query_selection": qe,
            "query_key_sel": bf(f64(qk) * f64(qe)),
            "memory_shrinkage": ms,
            "memory_value": bf(np.random.standard_normal((B, C, N)) * g / s[None, None, :])}


def reference(memory_key, memory_key_sq, query_key, query_selection, query_key_sel, memory_shrinkage, memory_value):
    qe = f64(query_selection)
    qs = f64(query_key_sel)
    ms = f64(memory_shrinkage)[:, :, None]
    a_sq = f64(memory_key_sq).transpose(0, 2, 1) @ qe
    two_ab = 2.0 * (f64(memory_key).transpose(0, 2, 1) @ qs)
    b_sq = np.sum(qs * f64(query_key), axis=1, keepdims=True)
    similarity = (-a_sq + two_ab - b_sq) * ms * (1.0 / np.sqrt(CK))
    e = np.exp(similarity - similarity.max(axis=1, keepdims=True))
    affinity = e / e.sum(axis=1, keepdims=True)
    return mxq(f64(memory_value), 2, "e4m3") @ mxq(affinity, 1, "e4m3")

@@ -1,0 +1,294 @@
+import math
+from contextlib import ExitStack
+
+import concourse.mybir as mybir
+from concourse.masks import make_identity
+
+F32 = mybir.dt.float32
+BF16 = mybir.dt.bfloat16
+U32 = mybir.dt.uint32
+U8 = mybir.dt.uint8
+FP8X4 = mybir.dt.float8_e4m3fn_x4
+ALU = mybir.AluOpType
+ACT = mybir.ActivationFunctionType
+AXIS = mybir.AxisListType
+
+P = 128
+KEY_CHANNELS = 128
+MEMORY = 2048
+QUERIES = 512
+VALUE_CHANNELS = 1536
+PACK = 4
+K_PASS = P * PACK
+PASSES = MEMORY // K_PASS
+QUERY_TILES = QUERIES // P
+VALUE_TILES = VALUE_CHANNELS // P
+BANK = 512
+TILES_PER_BANK = BANK // P
+VALUE_BANKS = VALUE_TILES // TILES_PER_BANK
+ROUNDS = QUERY_TILES + 2
+
+INV_SQRT_CK = 1.0 / math.sqrt(KEY_CHANNELS)
+
+FLOPS = 2 * VALUE_CHANNELS * MEMORY * QUERIES + 2 * 2 * KEY_CHANNELS * MEMORY * QUERIES
+
+
+def pass_order(columns):
+    return columns.rearrange("c (u q e) -> c u e q", u=2, e=2)
+
+
+def tile_vidsam_pa_kernel(
+    tc,
+    memory_key,
+    memory_key_sq,
+    query_key,
+    query_selection,
+    query_key_sel,
+    memory_shrinkage,
+    memory_value,
+    out,
+):
+    nc = tc.nc
+    with ExitStack() as stack:
+        const = stack.enter_context(tc.tile_pool(name="const", bufs=1))
+        raw_pool = stack.enter_context(tc.tile_pool(name="raw", bufs=VALUE_TILES))
+        work = stack.enter_context(tc.tile_pool(name="work", bufs=2))
+        small = stack.enter_context(tc.tile_pool(name="small", bufs=4))
+        stage = stack.enter_context(tc.tile_pool(name="stage", bufs=4))
+        psum_sim = stack.enter_context(tc.psum_pool(name="psum_sim", bufs=2))
+        psum_tr = stack.enter_context(tc.psum_pool(name="psum_tr", bufs=4))
+        psum_acc = stack.enter_context(tc.psum_pool(name="psum_acc", bufs=2))
+        stack.enter_context(tc.manual_schedule())
+
+        qs = const.tile([P, QUERIES], BF16)
+        nc.sync.dma_start(out=qs[:], in_=query_key_sel.flatten_outer_dims())
+        qk = const.tile([P, QUERIES], BF16)
+        nc.sync.dma_start(out=qk[:], in_=query_key.flatten_outer_dims())
+        qe = const.tile([P, QUERIES], BF16)
+        nc.sync.dma_start(out=qe[:], in_=query_selection.flatten_outer_dims())
+        mksq = const.tile([P, MEMORY], BF16)
+        nc.sync.dma_start(out=mksq[:], in_=memory_key_sq.flatten_outer_dims())
+        mk = const.tile([P, MEMORY], BF16)
+        nc.sync.dma_start(out=mk[:], in_=memory_key.flatten_outer_dims())
+
+        shrink_row = const.tile([P, MEMORY], BF16)
+        nc.vector.memset(shrink_row[:], 0.0)
+        nc.scalar.dma_start(out=shrink_row[0:1, :], in_=memory_shrinkage)
+
+        values = memory_value.flatten_outer_dims()
+        raw_tiles = []
+        for m in range(VALUE_TILES):
+            raw = raw_pool.tile([P, MEMORY], BF16, name="raw")
+            nc.sync.dma_start(out=raw[:], in_=values[m * P : (m + 1) * P, :])
+            raw_tiles.append(raw)
+
+        zero_col = const.tile([P, 1], F32)
+        nc.vector.memset(zero_col[:], 0.0)
+        one_col = const.tile([P, 1], F32)
+        nc.scalar.activation(out=one_col[:], in_=zero_col[:], func=ACT.Exp)
+        ident_f32 = const.tile([P, P], F32)
+        make_identity(nc, ident_f32[:])
+        ident_bf16 = const.tile([P, P], BF16)
+        make_identity(nc, ident_bf16[:])
+        ones_bf16 = const.tile([P, P], BF16)
+        nc.vector.memset(ones_bf16[:], 1.0)
+        ones_f32 = const.tile([P, 2], F32)
+        nc.vector.memset(ones_f32[:], 1.0)
+
+        qs_m2 = const.tile([P, QUERIES], BF16)
+        nc.vector.tensor_scalar(out=qs_m2[:], in0=qs[:], scalar1=-2.0, scalar2=None, op0=ALU.mult)
+        qs_qk = const.tile([P, QUERIES], F32)
+        nc.vector.tensor_tensor(out=qs_qk[:], in0=qs[:], in1=qk[:], op=ALU.mult)
+        b_sq_bank = psum_sim.tile([P, QUERY_TILES, 2], F32, tag="sim")
+        for i in range(QUERY_TILES):
+            nc.tensor.matmul(
+                out=b_sq_bank[:, i, :],
+                lhsT=qs_qk[:, i * P : (i + 1) * P],
+                rhs=ones_f32[:],
+                start=True,
+                stop=True,
+            )
+        b_sq = const.tile([P, QUERY_TILES], F32)
+        nc.vector.tensor_copy(out=b_sq[:], in_=b_sq_bank[:, :, 0])
+
+        shrink = const.tile([P, MEMORY], BF16)
+        for g in range(PASSES):
+            cols = slice(g * K_PASS, (g + 1) * K_PASS)
+            spread = psum_sim.tile([P, 2, 2, P], F32, tag="sim")
+            nc.tensor.matmul(
+                out=spread[:], lhsT=ones_bf16[:], rhs=pass_order(shrink_row[:, cols]), start=True, stop=True
+            )
+            nc.scalar.copy(out=shrink[:, cols], in_=spread[:].rearrange("p u e q -> p (u e q)"))
+
+        value_codes = const.tile([P, VALUE_TILES, PASSES, P], U32, align_bytes=64)
+        value_scales = const.tile([P, VALUE_TILES, PASSES, P], U8, align_bytes=64)
+        aff_codes = const.tile([P, QUERY_TILES, PASSES, P], U32, align_bytes=64)
+        aff_scales = const.tile([P, QUERY_TILES, PASSES, P], U8, align_bytes=64)
+        out_view = out.flatten_outer_dims().rearrange("(m c) p -> c m p", c=P)
+
+        scaled = {}
+        shift = {}
+        expo = {}
+        total = {}
+        aff = {}
+        aff_grouped = {}
+        value_grouped = {}
+
+        def distances(i, g):
+            if not 0 <= i < QUERY_TILES:
+                return
+            if g == 0:
+                scaled[i] = work.tile([P, MEMORY], F32, name="scaled")
+            cols = slice(g * K_PASS, (g + 1) * K_PASS)
+            dist = psum_sim.tile([P, 2, 2, P], F32, tag="sim")
+            nc.tensor.matmul(
+                out=dist[:], lhsT=qe[:, i * P : (i + 1) * P], rhs=pass_order(mksq[:, cols]), start=True, stop=False
+            )
+            nc.tensor.matmul(
+                out=dist[:], lhsT=qs_m2[:, i * P : (i + 1) * P], rhs=pass_order(mk[:, cols]), start=False, stop=True
+            )
+            nc.vector.scalar_tensor_tensor(
+                out=scaled[i][:, cols],
+                in0=dist[:].rearrange("p u e q -> p (u e q)"),
+                scalar=b_sq[:, i : i + 1],
+                in1=shrink[:, cols],
+                op0=ALU.add,
+                op1=ALU.mult,
+            )
+
+        def minimum(i):
+            if not 0 <= i < QUERY_TILES:
+                return
+            least = small.tile([P, 1], F32, name="least")
+            nc.vector.tensor_reduce(out=least[:], in_=scaled[i][:], axis=AXIS.X, op=ALU.min)
+            shift[i] = small.tile([P, 1], F32, name="shift")
+            nc.vector.tensor_scalar(out=shift[i][:], in0=least[:], scalar1=INV_SQRT_CK, scalar2=None, op0=ALU.mult)
+
+        def exponentials(i):
+            if not 0 <= i < QUERY_TILES:
+                return
+            expo[i] = work.tile([P, MEMORY], F32, name="expo")
+            total[i] = small.tile([P, 1], F32, name="total")
+            nc.scalar.activation(
+                out=expo[i][:],
+                in_=scaled[i][:],
+                func=ACT.Exp,
+                bias=shift[i][:],
+                scale=-INV_SQRT_CK,
+                accum_out=total[i][:],
+            )
+
+        def normalise(i):
+            if not 0 <= i < QUERY_TILES:
+                return
+            inverse = small.tile([P, 1], F32, name="inverse")
+            nc.vector.reciprocal(out=inverse[:], in_=total[i][:])
+            aff[i] = work.tile([P, MEMORY], BF16, name="aff")
+            nc.vector.tensor_scalar(out=aff[i][:], in0=expo[i][:], scalar1=inverse[:], scalar2=None, op0=ALU.mult)
+
+        def turn_affinity(i, half):
+            if not 0 <= i < QUERY_TILES:
+                return
+            if half == 0:
+                aff_grouped[i] = work.tile([P, PASSES, P, PACK], BF16, name="aff_grouped", align_bytes=64)
+            turned = psum_tr.tile([P, 2, PACK, P], BF16, tag="turned")
+            for gl in range(2):
+                for t in range(PACK):
+                    first = (2 * half + gl) * K_PASS + t * P
+                    nc.tensor.transpose(turned[:, gl, t, :], aff[i][:, first : first + P], ident_bf16[:])
+            nc.scalar.copy(
+                out=aff_grouped[i][:, 2 * half : 2 * half + 2, :, :],
+                in_=turned[:].rearrange("q g t p -> q g p t"),
+            )
+
+        def quantise_affinity(i):
+            if not 0 <= i < QUERY_TILES:
+                return
+            nc.vector.quantize_mx(
+                out=aff_codes[:, i, :, :].rearrange("q g p -> q (g p)").bitcast(FP8X4),
+                scales=aff_scales[:, i, :, :].rearrange("q g p -> q (g p)"),
+                in_=aff_grouped[i][:].rearrange("q g p t -> q (g p t)"),
+            )
+
+        def turn_values(m):
+            if not 0 <= m < VALUE_TILES:
+                return
+            words = raw_tiles[m][:].bitcast(F32)
+            value_grouped[m] = stage.tile([P, PASSES, P, 2], F32, name="value_grouped", align_bytes=64)
+            for half in range(2):
+                turned = psum_tr.tile([P, 2, 2, P], F32, tag="turned")
+                for gl in range(2):
+                    for u in range(2):
+                        first = ((2 * half + gl) * 2 + u) * P
+                        nc.tensor.transpose(turned[:, gl, u, :], words[:, first : first + P], ident_f32[:])
+                nc.scalar.copy(
+                    out=value_grouped[m][:, 2 * half : 2 * half + 2, :, :],
+                    in_=turned[:].rearrange("q g u c -> q g c u"),
+                )
+
+        def quantise_values(m):
+            if not 0 <= m < VALUE_TILES:
+                return
+            nc.vector.quantize_mx(
+                out=value_codes[:, m, :, :].rearrange("q g c -> q (g c)").bitcast(FP8X4),
+                scales=value_scales[:, m, :, :].rearrange("q g c -> q (g c)"),
+                in_=value_grouped[m][:].rearrange("q g c u -> q (g c u)").bitcast(BF16),
+            )
+
+        def products(r, k):
+            due = [
+                (i, b)
+                for i in range(QUERY_TILES)
+                for b in range(VALUE_BANKS)
+                if max(i + 2, b + 1) == r
+            ]
+            if k >= len(due):
+                return
+            i, b = due[k]
+            acc = psum_acc.tile([P, TILES_PER_BANK, P], F32, tag="acc")
+            for cell in range(TILES_PER_BANK):
+                m = b * TILES_PER_BANK + cell
+                for g in range(PASSES):
+                    nc.tensor.matmul_mx(
+                        out=acc[:, cell, :],
+                        lhsT=value_codes[:, m, g, :].bitcast(FP8X4),
+                        lhsT_scale=value_scales[:, m, g, :],
+                        rhs=aff_codes[:, i, g, :].bitcast(FP8X4),
+                        rhs_scale=aff_scales[:, i, g, :],
+                        start=(g == 0),
+                        stop=(g == PASSES - 1),
+                    )
+            result = stage.tile([P, TILES_PER_BANK, P], F32, name="result")
+            if b % 2 == 0:
+                nc.vector.tensor_copy(out=result[:], in_=acc[:])
+            else:
+                nc.scalar.copy(out=result[:], in_=acc[:])
+            nc.sync.dma_start(
+                out=out_view[:, b * TILES_PER_BANK : (b + 1) * TILES_PER_BANK, i * P : (i + 1) * P],
+                in_=result[:],
+            )
+
+        for r in range(ROUNDS):
+            m0 = r * TILES_PER_BANK
+            distances(r, 0)
+            distances(r, 1)
+            quantise_values(m0 - 2)
+            turn_values(m0)
+            distances(r, 2)
+            normalise(r - 1)
+            quantise_values(m0 - 1)
+            distances(r, 3)
+            products(r, 0)
+            turn_values(m0 + 1)
+            turn_values(m0 + 2)
+            minimum(r)
+            quantise_values(m0)
+            turn_affinity(r - 1, 0)
+            turn_affinity(r - 1, 1)
+            quantise_values(m0 + 1)
+            turn_values(m0 + 3)
+            exponentials(r)
+            products(r, 1)
+            quantise_affinity(r - 1)
+            products(r, 2)
+            products(r, 3)

@@ -21,6 +21,7 @@ VALUE_CHANNELS = 1536
 PACK = 4
 K_PASS = P * PACK
 PASSES = MEMORY // K_PASS
+HALF = MEMORY // 2
 QUERY_TILES = QUERIES // P
 VALUE_TILES = VALUE_CHANNELS // P
 BANK = 512
@@ -60,6 +61,8 @@ def tile_vidsam_pa_kernel(
         psum_acc = stack.enter_context(tc.psum_pool(name="psum_acc", bufs=2))
         stack.enter_context(tc.manual_schedule())
 
+        shrink_in = const.tile([1, MEMORY], BF16)
+        nc.sync.dma_start(out=shrink_in[:], in_=memory_shrinkage)
         qs = const.tile([P, QUERIES], BF16)
         nc.sync.dma_start(out=qs[:], in_=query_key_sel.flatten_outer_dims())
         qk = const.tile([P, QUERIES], BF16)
@@ -67,14 +70,11 @@ def tile_vidsam_pa_kernel(
         qe = const.tile([P, QUERIES], BF16)
         nc.sync.dma_start(out=qe[:], in_=query_selection.flatten_outer_dims())
         mksq = const.tile([P, MEMORY], BF16)
-        nc.sync.dma_start(out=mksq[:], in_=memory_key_sq.flatten_outer_dims())
         mk = const.tile([P, MEMORY], BF16)
-        nc.sync.dma_start(out=mk[:], in_=memory_key.flatten_outer_dims())
-
-        shrink_row = const.tile([P, MEMORY], BF16)
-        nc.vector.memset(shrink_row[:], 0.0)
-        nc.scalar.dma_start(out=shrink_row[0:1, :], in_=memory_shrinkage)
-
+        for h in range(2):
+            cols = slice(h * HALF, (h + 1) * HALF)
+            nc.sync.dma_start(out=mksq[:, cols], in_=memory_key_sq.flatten_outer_dims()[:, cols])
+            nc.sync.dma_start(out=mk[:, cols], in_=memory_key.flatten_outer_dims()[:, cols])
         values = memory_value.flatten_outer_dims()
         raw_tiles = []
         for m in range(VALUE_TILES):
@@ -82,6 +82,9 @@ def tile_vidsam_pa_kernel(
             nc.sync.dma_start(out=raw[:], in_=values[m * P : (m + 1) * P, :])
             raw_tiles.append(raw)
 
+        shrink_row = const.tile([P, MEMORY], BF16)
+        nc.gpsimd.memset(shrink_row[:].bitcast(F32), 0.0)
+        nc.vector.tensor_copy(out=shrink_row[0:1, :], in_=shrink_in[:])
         zero_col = const.tile([P, 1], F32)
         nc.vector.memset(zero_col[:], 0.0)
         one_col = const.tile([P, 1], F32)
@@ -99,26 +102,8 @@ def tile_vidsam_pa_kernel(
         nc.vector.tensor_scalar(out=qs_m2[:], in0=qs[:], scalar1=-2.0, scalar2=None, op0=ALU.mult)
         qs_qk = const.tile([P, QUERIES], F32)
         nc.vector.tensor_tensor(out=qs_qk[:], in0=qs[:], in1=qk[:], op=ALU.mult)
-        b_sq_bank = psum_sim.tile([P, QUERY_TILES, 2], F32, tag="sim")
-        for i in range(QUERY_TILES):
-            nc.tensor.matmul(
-                out=b_sq_bank[:, i, :],
-                lhsT=qs_qk[:, i * P : (i + 1) * P],
-                rhs=ones_f32[:],
-                start=True,
-                stop=True,
-            )
         b_sq = const.tile([P, QUERY_TILES], F32)
-        nc.vector.tensor_copy(out=b_sq[:], in_=b_sq_bank[:, :, 0])
-
         shrink = const.tile([P, MEMORY], BF16)
-        for g in range(PASSES):
-            cols = slice(g * K_PASS, (g + 1) * K_PASS)
-            spread = psum_sim.tile([P, 2, 2, P], F32, tag="sim")
-            nc.tensor.matmul(
-                out=spread[:], lhsT=ones_bf16[:], rhs=pass_order(shrink_row[:, cols]), start=True, stop=True
-            )
-            nc.scalar.copy(out=shrink[:, cols], in_=spread[:].rearrange("p u e q -> p (u e q)"))
 
         value_codes = const.tile([P, VALUE_TILES, PASSES, P], U32, align_bytes=64)
         value_scales = const.tile([P, VALUE_TILES, PASSES, P], U8, align_bytes=64)
@@ -130,9 +115,30 @@ def tile_vidsam_pa_kernel(
         shift = {}
         expo = {}
         total = {}
+        inverse = {}
         aff = {}
         aff_grouped = {}
         value_grouped = {}
+
+        def query_norms():
+            b_sq_bank = psum_acc.tile([P, QUERY_TILES, 2], F32, tag="acc")
+            for i in range(QUERY_TILES):
+                nc.tensor.matmul(
+                    out=b_sq_bank[:, i, :],
+                    lhsT=qs_qk[:, i * P : (i + 1) * P],
+                    rhs=ones_f32[:],
+                    start=True,
+                    stop=True,
+                )
+            nc.vector.tensor_copy(out=b_sq[:], in_=b_sq_bank[:, :, 0])
+
+        def spread_shrinkage(g):
+            cols = slice(g * K_PASS, (g + 1) * K_PASS)
+            spread = psum_tr.tile([P, 2, 2, P], F32, tag="turned")
+            nc.tensor.matmul(
+                out=spread[:], lhsT=ones_bf16[:], rhs=pass_order(shrink_row[:, cols]), start=True, stop=True
+            )
+            nc.scalar.copy(out=shrink[:, cols], in_=spread[:].rearrange("p u e q -> p (u e q)"))
 
         def distances(i, g):
             if not 0 <= i < QUERY_TILES:
@@ -178,13 +184,17 @@ def tile_vidsam_pa_kernel(
                 accum_out=total[i][:],
             )
 
-        def normalise(i):
+        def normalise(i, half):
             if not 0 <= i < QUERY_TILES:
                 return
-            inverse = small.tile([P, 1], F32, name="inverse")
-            nc.vector.reciprocal(out=inverse[:], in_=total[i][:])
-            aff[i] = work.tile([P, MEMORY], BF16, name="aff")
-            nc.vector.tensor_scalar(out=aff[i][:], in0=expo[i][:], scalar1=inverse[:], scalar2=None, op0=ALU.mult)
+            if half == 0:
+                inverse[i] = small.tile([P, 1], F32, name="inverse")
+                nc.vector.reciprocal(out=inverse[i][:], in_=total[i][:])
+                aff[i] = work.tile([P, MEMORY], BF16, name="aff")
+            cols = slice(half * HALF, (half + 1) * HALF)
+            nc.vector.tensor_scalar(
+                out=aff[i][:, cols], in0=expo[i][:, cols], scalar1=inverse[i][:], scalar2=None, op0=ALU.mult
+            )
 
         def turn_affinity(i, half):
             if not 0 <= i < QUERY_TILES:
@@ -201,13 +211,14 @@ def tile_vidsam_pa_kernel(
                 in_=turned[:].rearrange("q g t p -> q g p t"),
             )
 
-        def quantise_affinity(i):
+        def quantise_affinity(i, half):
             if not 0 <= i < QUERY_TILES:
                 return
+            two = slice(2 * half, 2 * half + 2)
             nc.vector.quantize_mx(
-                out=aff_codes[:, i, :, :].rearrange("q g p -> q (g p)").bitcast(FP8X4),
-                scales=aff_scales[:, i, :, :].rearrange("q g p -> q (g p)"),
-                in_=aff_grouped[i][:].rearrange("q g p t -> q (g p t)"),
+                out=aff_codes[:, i, two, :].rearrange("q g p -> q (g p)").bitcast(FP8X4),
+                scales=aff_scales[:, i, two, :].rearrange("q g p -> q (g p)"),
+                in_=aff_grouped[i][:, two, :, :].rearrange("q g p t -> q (g p t)"),
             )
 
         def turn_values(m):
@@ -235,16 +246,7 @@ def tile_vidsam_pa_kernel(
                 in_=value_grouped[m][:].rearrange("q g c u -> q (g c u)").bitcast(BF16),
             )
 
-        def products(r, k):
-            due = [
-                (i, b)
-                for i in range(QUERY_TILES)
-                for b in range(VALUE_BANKS)
-                if max(i + 2, b + 1) == r
-            ]
-            if k >= len(due):
-                return
-            i, b = due[k]
+        def product(i, b, copy_engine):
             acc = psum_acc.tile([P, TILES_PER_BANK, P], F32, tag="acc")
             for cell in range(TILES_PER_BANK):
                 m = b * TILES_PER_BANK + cell
@@ -259,7 +261,7 @@ def tile_vidsam_pa_kernel(
                         stop=(g == PASSES - 1),
                     )
             result = stage.tile([P, TILES_PER_BANK, P], F32, name="result")
-            if b % 2 == 0:
+            if copy_engine == "vector":
                 nc.vector.tensor_copy(out=result[:], in_=acc[:])
             else:
                 nc.scalar.copy(out=result[:], in_=acc[:])
@@ -268,27 +270,42 @@ def tile_vidsam_pa_kernel(
                 in_=result[:],
             )
 
+        def products(r, k):
+            due = sorted((b, i) for i in range(QUERY_TILES) for b in range(VALUE_BANKS) if max(i + 2, b + 1) == r)
+            if k < len(due):
+                b, i = due[k]
+                product(i, b, "scalar" if k == 0 else "vector")
+
+        def first_distances(r, g):
+            if r == 0:
+                spread_shrinkage(g)
+            if r == 0 and g == 0:
+                query_norms()
+            distances(r, g)
+
         for r in range(ROUNDS):
             m0 = r * TILES_PER_BANK
-            distances(r, 0)
-            distances(r, 1)
+            first_distances(r, 0)
             quantise_values(m0 - 2)
             turn_values(m0)
-            distances(r, 2)
-            normalise(r - 1)
             quantise_values(m0 - 1)
-            distances(r, 3)
-            products(r, 0)
+            first_distances(r, 1)
             turn_values(m0 + 1)
-            turn_values(m0 + 2)
-            minimum(r)
+            normalise(r - 1, 0)
+            normalise(r - 1, 1)
             quantise_values(m0)
+            products(r, 0)
+            first_distances(r, 2)
+            first_distances(r, 3)
+            turn_values(m0 + 2)
             turn_affinity(r - 1, 0)
+            minimum(r)
             turn_affinity(r - 1, 1)
-            quantise_values(m0 + 1)
+            products(r, 1)
             turn_values(m0 + 3)
             exponentials(r)
-            products(r, 1)
-            quantise_affinity(r - 1)
+            quantise_affinity(r - 1, 0)
+            quantise_affinity(r - 1, 1)
+            quantise_values(m0 + 1)
             products(r, 2)
             products(r, 3)

@@ -71,37 +71,46 @@ def tile_vidsam_pa_kernel(
         nc.sync.dma_start(out=qe[:], in_=query_selection.flatten_outer_dims())
         mksq = const.tile([P, MEMORY], BF16)
         mk = const.tile([P, MEMORY], BF16)
-        for h in range(2):
+        values = memory_value.flatten_outer_dims()
+        raw_tiles = []
+
+        def load_keys(h):
             cols = slice(h * HALF, (h + 1) * HALF)
             nc.sync.dma_start(out=mksq[:, cols], in_=memory_key_sq.flatten_outer_dims()[:, cols])
             nc.sync.dma_start(out=mk[:, cols], in_=memory_key.flatten_outer_dims()[:, cols])
-        values = memory_value.flatten_outer_dims()
-        raw_tiles = []
-        for m in range(VALUE_TILES):
+
+        def load_values(m):
             raw = raw_pool.tile([P, MEMORY], BF16, name="raw")
             nc.sync.dma_start(out=raw[:], in_=values[m * P : (m + 1) * P, :])
             raw_tiles.append(raw)
 
+        load_keys(0)
+        load_values(0)
+        load_keys(1)
+        for m in range(1, VALUE_TILES):
+            load_values(m)
+
         shrink_row = const.tile([P, MEMORY], BF16)
         nc.gpsimd.memset(shrink_row[:].bitcast(F32), 0.0)
-        nc.vector.tensor_copy(out=shrink_row[0:1, :], in_=shrink_in[:])
-        zero_col = const.tile([P, 1], F32)
-        nc.vector.memset(zero_col[:], 0.0)
-        one_col = const.tile([P, 1], F32)
-        nc.scalar.activation(out=one_col[:], in_=zero_col[:], func=ACT.Exp)
-        ident_f32 = const.tile([P, P], F32)
-        make_identity(nc, ident_f32[:])
-        ident_bf16 = const.tile([P, P], BF16)
-        make_identity(nc, ident_bf16[:])
         ones_bf16 = const.tile([P, P], BF16)
         nc.vector.memset(ones_bf16[:], 1.0)
         ones_f32 = const.tile([P, 2], F32)
         nc.vector.memset(ones_f32[:], 1.0)
+        zero_col = const.tile([P, 1], F32)
+        nc.vector.memset(zero_col[:], 0.0)
+        one_col = const.tile([P, 1], F32)
+        nc.scalar.activation(out=one_col[:], in_=zero_col[:], func=ACT.Exp)
+        nc.vector.tensor_copy(out=shrink_row[0:1, :], in_=shrink_in[:])
+        ident_f32 = const.tile([P, P], F32)
+        make_identity(nc, ident_f32[:])
+        ident_bf16 = const.tile([P, P], BF16)
+        make_identity(nc, ident_bf16[:])
 
         qs_m2 = const.tile([P, QUERIES], BF16)
         nc.vector.tensor_scalar(out=qs_m2[:], in0=qs[:], scalar1=-2.0, scalar2=None, op0=ALU.mult)
         qs_qk = const.tile([P, QUERIES], F32)
-        nc.vector.tensor_tensor(out=qs_qk[:], in0=qs[:], in1=qk[:], op=ALU.mult)
+        nc.vector.tensor_tensor(out=qs_qk[:, 0:P], in0=qs[:, 0:P], in1=qk[:, 0:P], op=ALU.mult)
+        nc.vector.tensor_tensor(out=qs_qk[:, P:], in0=qs[:, P:], in1=qk[:, P:], op=ALU.mult)
         b_sq = const.tile([P, QUERY_TILES], F32)
         shrink = const.tile([P, MEMORY], BF16)
 
@@ -120,9 +129,9 @@ def tile_vidsam_pa_kernel(
         aff_grouped = {}
         value_grouped = {}
 
-        def query_norms():
+        def query_norms(first, last):
             b_sq_bank = psum_acc.tile([P, QUERY_TILES, 2], F32, tag="acc")
-            for i in range(QUERY_TILES):
+            for i in range(first, last):
                 nc.tensor.matmul(
                     out=b_sq_bank[:, i, :],
                     lhsT=qs_qk[:, i * P : (i + 1) * P],
@@ -130,7 +139,7 @@ def tile_vidsam_pa_kernel(
                     start=True,
                     stop=True,
                 )
-            nc.vector.tensor_copy(out=b_sq[:], in_=b_sq_bank[:, :, 0])
+            nc.vector.tensor_copy(out=b_sq[:, first:last], in_=b_sq_bank[:, first:last, 0])
 
         def spread_shrinkage(g):
             cols = slice(g * K_PASS, (g + 1) * K_PASS)
@@ -276,27 +285,25 @@ def tile_vidsam_pa_kernel(
                 b, i = due[k]
                 product(i, b, "scalar" if k == 0 else "vector")
 
-        def first_distances(r, g):
-            if r == 0:
-                spread_shrinkage(g)
-            if r == 0 and g == 0:
-                query_norms()
-            distances(r, g)
-
+        for g in range(PASSES):
+            spread_shrinkage(g)
+        query_norms(0, 1)
         for r in range(ROUNDS):
             m0 = r * TILES_PER_BANK
-            first_distances(r, 0)
+            distances(r, 0)
+            if r == 0:
+                query_norms(1, QUERY_TILES)
             quantise_values(m0 - 2)
             turn_values(m0)
             quantise_values(m0 - 1)
-            first_distances(r, 1)
+            distances(r, 1)
             turn_values(m0 + 1)
             normalise(r - 1, 0)
             normalise(r - 1, 1)
             quantise_values(m0)
             products(r, 0)
-            first_distances(r, 2)
-            first_distances(r, 3)
+            distances(r, 2)
+            distances(r, 3)
             turn_values(m0 + 2)
             turn_affinity(r - 1, 0)
             minimum(r)

@@ -112,7 +112,7 @@ def tile_vidsam_pa_kernel(
         nc.vector.tensor_tensor(out=qs_qk[:, 0:P], in0=qs[:, 0:P], in1=qk[:, 0:P], op=ALU.mult)
         nc.vector.tensor_tensor(out=qs_qk[:, P:], in0=qs[:, P:], in1=qk[:, P:], op=ALU.mult)
         b_sq = const.tile([P, QUERY_TILES], F32)
-        shrink = const.tile([P, MEMORY], BF16)
+        factor = const.tile([P, MEMORY], F32)
 
         value_codes = const.tile([P, VALUE_TILES, PASSES, P], U32, align_bytes=64)
         value_scales = const.tile([P, VALUE_TILES, PASSES, P], U8, align_bytes=64)
@@ -147,7 +147,7 @@ def tile_vidsam_pa_kernel(
             nc.tensor.matmul(
                 out=spread[:], lhsT=ones_bf16[:], rhs=pass_order(shrink_row[:, cols]), start=True, stop=True
             )
-            nc.scalar.copy(out=shrink[:, cols], in_=spread[:].rearrange("p u e q -> p (u e q)"))
+            nc.scalar.mul(out=factor[:, cols], in_=spread[:].rearrange("p u e q -> p (u e q)"), mul=-INV_SQRT_CK)
 
         def distances(i, g):
             if not 0 <= i < QUERY_TILES:
@@ -166,18 +166,16 @@ def tile_vidsam_pa_kernel(
                 out=scaled[i][:, cols],
                 in0=dist[:].rearrange("p u e q -> p (u e q)"),
                 scalar=b_sq[:, i : i + 1],
-                in1=shrink[:, cols],
+                in1=factor[:, cols],
                 op0=ALU.add,
                 op1=ALU.mult,
             )
 
-        def minimum(i):
+        def maximum(i):
             if not 0 <= i < QUERY_TILES:
                 return
-            least = small.tile([P, 1], F32, name="least")
-            nc.vector.tensor_reduce(out=least[:], in_=scaled[i][:], axis=AXIS.X, op=ALU.min)
             shift[i] = small.tile([P, 1], F32, name="shift")
-            nc.vector.tensor_scalar(out=shift[i][:], in0=least[:], scalar1=INV_SQRT_CK, scalar2=None, op0=ALU.mult)
+            nc.vector.tensor_reduce(out=shift[i][:], in_=scaled[i][:], axis=AXIS.X, op=ALU.max, negate=True)
 
         def exponentials(i):
             if not 0 <= i < QUERY_TILES:
@@ -189,16 +187,19 @@ def tile_vidsam_pa_kernel(
                 in_=scaled[i][:],
                 func=ACT.Exp,
                 bias=shift[i][:],
-                scale=-INV_SQRT_CK,
                 accum_out=total[i][:],
             )
+
+        def invert_total(i):
+            if not 0 <= i < QUERY_TILES:
+                return
+            inverse[i] = small.tile([P, 1], F32, name="inverse")
+            nc.vector.reciprocal(out=inverse[i][:], in_=total[i][:])
 
         def normalise(i, half):
             if not 0 <= i < QUERY_TILES:
                 return
             if half == 0:
-                inverse[i] = small.tile([P, 1], F32, name="inverse")
-                nc.vector.reciprocal(out=inverse[i][:], in_=total[i][:])
                 aff[i] = work.tile([P, MEMORY], BF16, name="aff")
             cols = slice(half * HALF, (half + 1) * HALF)
             nc.vector.tensor_scalar(
@@ -295,18 +296,19 @@ def tile_vidsam_pa_kernel(
                 query_norms(1, QUERY_TILES)
             quantise_values(m0 - 2)
             turn_values(m0)
-            quantise_values(m0 - 1)
             distances(r, 1)
+            invert_total(r - 1)
+            quantise_values(m0 - 1)
             turn_values(m0 + 1)
             normalise(r - 1, 0)
             normalise(r - 1, 1)
-            quantise_values(m0)
             products(r, 0)
             distances(r, 2)
             distances(r, 3)
+            quantise_values(m0)
             turn_values(m0 + 2)
             turn_affinity(r - 1, 0)
-            minimum(r)
+            maximum(r)
             turn_affinity(r - 1, 1)
             products(r, 1)
             turn_values(m0 + 3)

@@ -59,7 +59,6 @@ def tile_vidsam_pa_kernel(
         psum_sim = stack.enter_context(tc.psum_pool(name="psum_sim", bufs=2))
         psum_tr = stack.enter_context(tc.psum_pool(name="psum_tr", bufs=4))
         psum_acc = stack.enter_context(tc.psum_pool(name="psum_acc", bufs=2))
-        stack.enter_context(tc.manual_schedule())
 
         shrink_in = const.tile([1, MEMORY], BF16)
         nc.sync.dma_start(out=shrink_in[:], in_=memory_shrinkage)

import math
from contextlib import ExitStack

import concourse.mybir as mybir
from concourse.masks import make_identity

F32 = mybir.dt.float32
BF16 = mybir.dt.bfloat16
U32 = mybir.dt.uint32
U8 = mybir.dt.uint8
FP8X4 = mybir.dt.float8_e4m3fn_x4
ALU = mybir.AluOpType
ACT = mybir.ActivationFunctionType
AXIS = mybir.AxisListType

P = 128
KEY_CHANNELS = 128
MEMORY = 2048
QUERIES = 512
VALUE_CHANNELS = 1536
PACK = 4
K_PASS = P * PACK
PASSES = MEMORY // K_PASS
HALF = MEMORY // 2
QUERY_TILES = QUERIES // P
VALUE_TILES = VALUE_CHANNELS // P
BANK = 512
TILES_PER_BANK = BANK // P
VALUE_BANKS = VALUE_TILES // TILES_PER_BANK
ROUNDS = QUERY_TILES + 2

INV_SQRT_CK = 1.0 / math.sqrt(KEY_CHANNELS)

FLOPS = 2 * VALUE_CHANNELS * MEMORY * QUERIES + 2 * 2 * KEY_CHANNELS * MEMORY * QUERIES


def pass_order(columns):
    return columns.rearrange("c (u q e) -> c u e q", u=2, e=2)


def tile_vidsam_pa_kernel(
    tc,
    memory_key,
    memory_key_sq,
    query_key,
    query_selection,
    query_key_sel,
    memory_shrinkage,
    memory_value,
    out,
):
    nc = tc.nc
    with ExitStack() as stack:
        const = stack.enter_context(tc.tile_pool(name="const", bufs=1))
        raw_pool = stack.enter_context(tc.tile_pool(name="raw", bufs=VALUE_TILES))
        work = stack.enter_context(tc.tile_pool(name="work", bufs=2))
        small = stack.enter_context(tc.tile_pool(name="small", bufs=4))
        stage = stack.enter_context(tc.tile_pool(name="stage", bufs=4))
        psum_sim = stack.enter_context(tc.psum_pool(name="psum_sim", bufs=2))
        psum_tr = stack.enter_context(tc.psum_pool(name="psum_tr", bufs=4))
        psum_acc = stack.enter_context(tc.psum_pool(name="psum_acc", bufs=2))

        shrink_in = const.tile([1, MEMORY], BF16)
        nc.sync.dma_start(out=shrink_in[:], in_=memory_shrinkage)
        qs = const.tile([P, QUERIES], BF16)
        nc.sync.dma_start(out=qs[:], in_=query_key_sel.flatten_outer_dims())
        qk = const.tile([P, QUERIES], BF16)
        nc.sync.dma_start(out=qk[:], in_=query_key.flatten_outer_dims())
        qe = const.tile([P, QUERIES], BF16)
        nc.sync.dma_start(out=qe[:], in_=query_selection.flatten_outer_dims())
        mksq = const.tile([P, MEMORY], BF16)
        mk = const.tile([P, MEMORY], BF16)
        values = memory_value.flatten_outer_dims()
        raw_tiles = []

        def load_keys(h):
            cols = slice(h * HALF, (h + 1) * HALF)
            nc.sync.dma_start(out=mksq[:, cols], in_=memory_key_sq.flatten_outer_dims()[:, cols])
            nc.sync.dma_start(out=mk[:, cols], in_=memory_key.flatten_outer_dims()[:, cols])

        def load_values(m):
            raw = raw_pool.tile([P, MEMORY], BF16, name="raw")
            nc.sync.dma_start(out=raw[:], in_=values[m * P : (m + 1) * P, :])
            raw_tiles.append(raw)

        load_keys(0)
        load_values(0)
        load_keys(1)
        for m in range(1, VALUE_TILES):
            load_values(m)

        shrink_row = const.tile([P, MEMORY], BF16)
        nc.gpsimd.memset(shrink_row[:].bitcast(F32), 0.0)
        ones_bf16 = const.tile([P, P], BF16)
        nc.vector.memset(ones_bf16[:], 1.0)
        ones_f32 = const.tile([P, 2], F32)
        nc.vector.memset(ones_f32[:], 1.0)
        zero_col = const.tile([P, 1], F32)
        nc.vector.memset(zero_col[:], 0.0)
        one_col = const.tile([P, 1], F32)
        nc.scalar.activation(out=one_col[:], in_=zero_col[:], func=ACT.Exp)
        nc.vector.tensor_copy(out=shrink_row[0:1, :], in_=shrink_in[:])
        ident_f32 = const.tile([P, P], F32)
        make_identity(nc, ident_f32[:])
        ident_bf16 = const.tile([P, P], BF16)
        make_identity(nc, ident_bf16[:])

        qs_m2 = const.tile([P, QUERIES], BF16)
        nc.vector.tensor_scalar(out=qs_m2[:], in0=qs[:], scalar1=-2.0, scalar2=None, op0=ALU.mult)
        qs_qk = const.tile([P, QUERIES], F32)
        nc.vector.tensor_tensor(out=qs_qk[:, 0:P], in0=qs[:, 0:P], in1=qk[:, 0:P], op=ALU.mult)
        nc.vector.tensor_tensor(out=qs_qk[:, P:], in0=qs[:, P:], in1=qk[:, P:], op=ALU.mult)
        b_sq = const.tile([P, QUERY_TILES], F32)
        factor = const.tile([P, MEMORY], F32)

        value_codes = const.tile([P, VALUE_TILES, PASSES, P], U32, align_bytes=64)
        value_scales = const.tile([P, VALUE_TILES, PASSES, P], U8, align_bytes=64)
        aff_codes = const.tile([P, QUERY_TILES, PASSES, P], U32, align_bytes=64)
        aff_scales = const.tile([P, QUERY_TILES, PASSES, P], U8, align_bytes=64)
        out_view = out.flatten_outer_dims().rearrange("(m c) p -> c m p", c=P)

        scaled = {}
        shift = {}
        expo = {}
        total = {}
        inverse = {}
        aff = {}
        aff_grouped = {}
        value_grouped = {}

        def query_norms(first, last):
            b_sq_bank = psum_acc.tile([P, QUERY_TILES, 2], F32, tag="acc")
            for i in range(first, last):
                nc.tensor.matmul(
                    out=b_sq_bank[:, i, :],
                    lhsT=qs_qk[:, i * P : (i + 1) * P],
                    rhs=ones_f32[:],
                    start=True,
                    stop=True,
                )
            nc.vector.tensor_copy(out=b_sq[:, first:last], in_=b_sq_bank[:, first:last, 0])

        def spread_shrinkage(g):
            cols = slice(g * K_PASS, (g + 1) * K_PASS)
            spread = psum_tr.tile([P, 2, 2, P], F32, tag="turned")
            nc.tensor.matmul(
                out=spread[:], lhsT=ones_bf16[:], rhs=pass_order(shrink_row[:, cols]), start=True, stop=True
            )
            nc.scalar.mul(out=factor[:, cols], in_=spread[:].rearrange("p u e q -> p (u e q)"), mul=-INV_SQRT_CK)

        def distances(i, g):
            if not 0 <= i < QUERY_TILES:
                return
            if g == 0:
                scaled[i] = work.tile([P, MEMORY], F32, name="scaled")
            cols = slice(g * K_PASS, (g + 1) * K_PASS)
            dist = psum_sim.tile([P, 2, 2, P], F32, tag="sim")
            nc.tensor.matmul(
                out=dist[:], lhsT=qe[:, i * P : (i + 1) * P], rhs=pass_order(mksq[:, cols]), start=True, stop=False
            )
            nc.tensor.matmul(
                out=dist[:], lhsT=qs_m2[:, i * P : (i + 1) * P], rhs=pass_order(mk[:, cols]), start=False, stop=True
            )
            nc.vector.scalar_tensor_tensor(
                out=scaled[i][:, cols],
                in0=dist[:].rearrange("p u e q -> p (u e q)"),
                scalar=b_sq[:, i : i + 1],
                in1=factor[:, cols],
                op0=ALU.add,
                op1=ALU.mult,
            )

        def maximum(i):
            if not 0 <= i < QUERY_TILES:
                return
            shift[i] = small.tile([P, 1], F32, name="shift")
            nc.vector.tensor_reduce(out=shift[i][:], in_=scaled[i][:], axis=AXIS.X, op=ALU.max, negate=True)

        def exponentials(i):
            if not 0 <= i < QUERY_TILES:
                return
            expo[i] = work.tile([P, MEMORY], F32, name="expo")
            total[i] = small.tile([P, 1], F32, name="total")
            nc.scalar.activation(
                out=expo[i][:],
                in_=scaled[i][:],
                func=ACT.Exp,
                bias=shift[i][:],
                accum_out=total[i][:],
            )

        def invert_total(i):
            if not 0 <= i < QUERY_TILES:
                return
            inverse[i] = small.tile([P, 1], F32, name="inverse")
            nc.vector.reciprocal(out=inverse[i][:], in_=total[i][:])

        def normalise(i, half):
            if not 0 <= i < QUERY_TILES:
                return
            if half == 0:
                aff[i] = work.tile([P, MEMORY], BF16, name="aff")
            cols = slice(half * HALF, (half + 1) * HALF)
            nc.vector.tensor_scalar(
                out=aff[i][:, cols], in0=expo[i][:, cols], scalar1=inverse[i][:], scalar2=None, op0=ALU.mult
            )

        def turn_affinity(i, half):
            if not 0 <= i < QUERY_TILES:
                return
            if half == 0:
                aff_grouped[i] = work.tile([P, PASSES, P, PACK], BF16, name="aff_grouped", align_bytes=64)
            turned = psum_tr.tile([P, 2, PACK, P], BF16, tag="turned")
            for gl in range(2):
                for t in range(PACK):
                    first = (2 * half + gl) * K_PASS + t * P
                    nc.tensor.transpose(turned[:, gl, t, :], aff[i][:, first : first + P], ident_bf16[:])
            nc.scalar.copy(
                out=aff_grouped[i][:, 2 * half : 2 * half + 2, :, :],
                in_=turned[:].rearrange("q g t p -> q g p t"),
            )

        def quantise_affinity(i, half):
            if not 0 <= i < QUERY_TILES:
                return
            two = slice(2 * half, 2 * half + 2)
            nc.vector.quantize_mx(
                out=aff_codes[:, i, two, :].rearrange("q g p -> q (g p)").bitcast(FP8X4),
                scales=aff_scales[:, i, two, :].rearrange("q g p -> q (g p)"),
                in_=aff_grouped[i][:, two, :, :].rearrange("q g p t -> q (g p t)"),
            )

        def turn_values(m):
            if not 0 <= m < VALUE_TILES:
                return
            words = raw_tiles[m][:].bitcast(F32)
            value_grouped[m] = stage.tile([P, PASSES, P, 2], F32, name="value_grouped", align_bytes=64)
            for half in range(2):
                turned = psum_tr.tile([P, 2, 2, P], F32, tag="turned")
                for gl in range(2):
                    for u in range(2):
                        first = ((2 * half + gl) * 2 + u) * P
                        nc.tensor.transpose(turned[:, gl, u, :], words[:, first : first + P], ident_f32[:])
                nc.scalar.copy(
                    out=value_grouped[m][:, 2 * half : 2 * half + 2, :, :],
                    in_=turned[:].rearrange("q g u c -> q g c u"),
                )

        def quantise_values(m):
            if not 0 <= m < VALUE_TILES:
                return
            nc.vector.quantize_mx(
                out=value_codes[:, m, :, :].rearrange("q g c -> q (g c)").bitcast(FP8X4),
                scales=value_scales[:, m, :, :].rearrange("q g c -> q (g c)"),
                in_=value_grouped[m][:].rearrange("q g c u -> q (g c u)").bitcast(BF16),
            )

        def product(i, b, copy_engine):
            acc = psum_acc.tile([P, TILES_PER_BANK, P], F32, tag="acc")
            for cell in range(TILES_PER_BANK):
                m = b * TILES_PER_BANK + cell
                for g in range(PASSES):
                    nc.tensor.matmul_mx(
                        out=acc[:, cell, :],
                        lhsT=value_codes[:, m, g, :].bitcast(FP8X4),
                        lhsT_scale=value_scales[:, m, g, :],
                        rhs=aff_codes[:, i, g, :].bitcast(FP8X4),
                        rhs_scale=aff_scales[:, i, g, :],
                        start=(g == 0),
                        stop=(g == PASSES - 1),
                    )
            result = stage.tile([P, TILES_PER_BANK, P], F32, name="result")
            if copy_engine == "vector":
                nc.vector.tensor_copy(out=result[:], in_=acc[:])
            else:
                nc.scalar.copy(out=result[:], in_=acc[:])
            nc.sync.dma_start(
                out=out_view[:, b * TILES_PER_BANK : (b + 1) * TILES_PER_BANK, i * P : (i + 1) * P],
                in_=result[:],
            )

        def products(r, k):
            due = sorted((b, i) for i in range(QUERY_TILES) for b in range(VALUE_BANKS) if max(i + 2, b + 1) == r)
            if k < len(due):
                b, i = due[k]
                product(i, b, "scalar" if k == 0 else "vector")

        for g in range(PASSES):
            spread_shrinkage(g)
        query_norms(0, 1)
        for r in range(ROUNDS):
            m0 = r * TILES_PER_BANK
            distances(r, 0)
            if r == 0:
                query_norms(1, QUERY_TILES)
            quantise_values(m0 - 2)
            turn_values(m0)
            distances(r, 1)
            invert_total(r - 1)
            quantise_values(m0 - 1)
            turn_values(m0 + 1)
            normalise(r - 1, 0)
            normalise(r - 1, 1)
            products(r, 0)
            distances(r, 2)
            distances(r, 3)
            quantise_values(m0)
            turn_values(m0 + 2)
            turn_affinity(r - 1, 0)
            maximum(r)
            turn_affinity(r - 1, 1)
            products(r, 1)
            turn_values(m0 + 3)
            exponentials(r)
            quantise_affinity(r - 1, 0)
            quantise_affinity(r - 1, 1)
            quantise_values(m0 + 1)
            products(r, 2)
            products(r, 3)
